import numpy as np
import ml_dtypes

BF16 = ml_dtypes.bfloat16


def bf(x):
    return np.asarray(x, np.float32).astype(BF16)


def f32(x):
    return np.asarray(x, np.float32)


def f64(x):
    return np.asarray(x).astype(np.float64)


def striped(idx):
    return np.tile(idx.reshape(-1, 16).T, (8, 1))


W, K, C, S, N = 2, 256, 128, 1024, 512


def setup_inputs():
    return {"x": bf(np.random.standard_normal((W, K, N))), "weight": bf(np.random.standard_normal((W, K, C)) / np.sqrt(W * K)), "bias": f32(np.random.standard_normal((W, C, N))), "base": f32(np.random.standard_normal((C, S))), "offs": striped(np.random.permutation(S)[:N])}


def reference(x, weight, bias, base, offs):
    idx = offs[:16].T.reshape(-1)
    y = np.einsum("rkc,rkn->cn", f64(weight), f64(x)) + f64(bias).sum(axis=0)
    res = f64(base).copy()
    res[:, idx] = y
    return res

@@ -1,0 +1,43 @@
+import concourse.mybir as mybir
+
+BF16, F32, U16 = mybir.dt.bfloat16, mybir.dt.float32, mybir.dt.uint16
+
+P = 128
+R, K = 2, 256
+N, S = 512, 1024
+BLOCKS = R * K // P
+
+FLOPS = 2 * R * K * P * N
+
+
+def tile_gemmrstritonpcie_kernel(tc, x, weight, bias, base, offs, out):
+    nc = tc.nc
+    with tc.tile_pool(name="held", bufs=1) as held, tc.psum_pool(name="psum", bufs=1) as psum:
+        offsets = held.tile([P, N // 16], U16, name="offsets")
+        nc.sync.dma_start(offsets[:], offs)
+
+        x_blocks = held.tile([P, BLOCKS, N], BF16, name="x_blocks")
+        nc.sync.dma_start(x_blocks[:], x.flatten_outer_dims().rearrange("(b p) n -> p b n", p=P))
+        weight_blocks = held.tile([P, BLOCKS, P], BF16, name="weight_blocks")
+        nc.scalar.dma_start(weight_blocks[:], weight.flatten_outer_dims().rearrange("(b p) c -> p b c", p=P))
+
+        both_biases = held.tile([P, R, N], F32, name="both_biases")
+        nc.scalar.dma_start(both_biases[:], bias.rearrange("r c n -> c r n"))
+        window = held.tile([P, S], F32, name="window")
+        nc.sync.dma_start(window[:], base)
+
+        products = psum.tile([P, N], F32, name="products")
+        for b in range(BLOCKS):
+            nc.tensor.matmul(
+                products[:], weight_blocks[:, b, :], x_blocks[:, b, :], start=(b == 0), stop=(b == BLOCKS - 1)
+            )
+
+        products_sb = held.tile([P, N], F32, name="products_sb")
+        nc.scalar.activation(products_sb[:], products[:], mybir.ActivationFunctionType.Copy)
+
+        bias_sum = held.tile([P, N], F32, name="bias_sum")
+        nc.vector.tensor_tensor(bias_sum[:], both_biases[:, 0, :], both_biases[:, 1, :], mybir.AluOpType.add)
+
+        nc.vector.tensor_tensor(window[:].indirect(offsets[:]), products_sb[:], bias_sum[:], mybir.AluOpType.add)
+
+        nc.sync.dma_start(out, window[:])

@@ -13,23 +13,28 @@ FLOPS = 2 * R * K * P * N
 def tile_gemmrstritonpcie_kernel(tc, x, weight, bias, base, offs, out):
     nc = tc.nc
     with tc.tile_pool(name="held", bufs=1) as held, tc.psum_pool(name="psum", bufs=1) as psum:
+
         offsets = held.tile([P, N // 16], U16, name="offsets")
         nc.sync.dma_start(offsets[:], offs)
 
-        x_blocks = held.tile([P, BLOCKS, N], BF16, name="x_blocks")
-        nc.sync.dma_start(x_blocks[:], x.flatten_outer_dims().rearrange("(b p) n -> p b n", p=P))
         weight_blocks = held.tile([P, BLOCKS, P], BF16, name="weight_blocks")
-        nc.scalar.dma_start(weight_blocks[:], weight.flatten_outer_dims().rearrange("(b p) c -> p b c", p=P))
+        nc.sync.dma_start(weight_blocks[:], weight.flatten_outer_dims().rearrange("(b p) c -> p b c", p=P))
+        x_by_block = x.flatten_outer_dims().rearrange("(b p) n -> b p n", p=P)
+        x_blocks = []
+        for b in range(BLOCKS):
+            x_block = held.tile([P, N], BF16, name=f"x_block{b}")
+            nc.sync.dma_start(x_block[:], x_by_block[b])
+            x_blocks.append(x_block)
 
         both_biases = held.tile([P, R, N], F32, name="both_biases")
-        nc.scalar.dma_start(both_biases[:], bias.rearrange("r c n -> c r n"))
+        nc.sync.dma_start(both_biases[:], bias.rearrange("r c n -> c r n"))
         window = held.tile([P, S], F32, name="window")
         nc.sync.dma_start(window[:], base)
 
         products = psum.tile([P, N], F32, name="products")
         for b in range(BLOCKS):
             nc.tensor.matmul(
-                products[:], weight_blocks[:, b, :], x_blocks[:, b, :], start=(b == 0), stop=(b == BLOCKS - 1)
+                products[:], weight_blocks[:, b, :], x_blocks[b][:], start=(b == 0), stop=(b == BLOCKS - 1)
             )
 
         products_sb = held.tile([P, N], F32, name="products_sb")

@@ -6,6 +6,8 @@ P = 128
 R, K = 2, 256
 N, S = 512, 1024
 BLOCKS = R * K // P
+LOADS = 2
+PER_LOAD = BLOCKS // LOADS
 
 FLOPS = 2 * R * K * P * N
 
@@ -18,13 +20,13 @@ def tile_gemmrstritonpcie_kernel(tc, x, weight, bias, base, offs, out):
         nc.sync.dma_start(offsets[:], offs)
 
         weight_blocks = held.tile([P, BLOCKS, P], BF16, name="weight_blocks")
-        nc.sync.dma_start(weight_blocks[:], weight.flatten_outer_dims().rearrange("(b p) c -> p b c", p=P))
-        x_by_block = x.flatten_outer_dims().rearrange("(b p) n -> b p n", p=P)
+        nc.sync.dma_start(weight_blocks[:], weight.flatten_outer_dims().rearrange("(p b) c -> p b c", p=P))
+        x_by_load = x.flatten_outer_dims().rearrange("(p l b) n -> l p b n", p=P, l=LOADS)
         x_blocks = []
-        for b in range(BLOCKS):
-            x_block = held.tile([P, N], BF16, name=f"x_block{b}")
-            nc.sync.dma_start(x_block[:], x_by_block[b])
-            x_blocks.append(x_block)
+        for l in range(LOADS):
+            x_part = held.tile([P, PER_LOAD, N], BF16, name=f"x_part{l}")
+            nc.sync.dma_start(x_part[:], x_by_load[l])
+            x_blocks.extend(x_part[:, b, :] for b in range(PER_LOAD))
 
         both_biases = held.tile([P, R, N], F32, name="both_biases")
         nc.sync.dma_start(both_biases[:], bias.rearrange("r c n -> c r n"))
@@ -33,9 +35,7 @@ def tile_gemmrstritonpcie_kernel(tc, x, weight, bias, base, offs, out):
 
         products = psum.tile([P, N], F32, name="products")
         for b in range(BLOCKS):
-            nc.tensor.matmul(
-                products[:], weight_blocks[:, b, :], x_blocks[b][:], start=(b == 0), stop=(b == BLOCKS - 1)
-            )
+            nc.tensor.matmul(products[:], weight_blocks[:, b, :], x_blocks[b], start=(b == 0), stop=(b == BLOCKS - 1))
 
         products_sb = held.tile([P, N], F32, name="products_sb")
         nc.scalar.activation(products_sb[:], products[:], mybir.ActivationFunctionType.Copy)

@@ -8,6 +8,7 @@ N, S = 512, 1024
 BLOCKS = R * K // P
 LOADS = 2
 PER_LOAD = BLOCKS // LOADS
+HALF = N // 2
 
 FLOPS = 2 * R * K * P * N
 
@@ -33,15 +34,19 @@ def tile_gemmrstritonpcie_kernel(tc, x, weight, bias, base, offs, out):
         window = held.tile([P, S], F32, name="window")
         nc.sync.dma_start(window[:], base)
 
-        products = psum.tile([P, N], F32, name="products")
-        for b in range(BLOCKS):
-            nc.tensor.matmul(products[:], weight_blocks[:, b, :], x_blocks[b], start=(b == 0), stop=(b == BLOCKS - 1))
-
-        products_sb = held.tile([P, N], F32, name="products_sb")
-        nc.scalar.activation(products_sb[:], products[:], mybir.ActivationFunctionType.Copy)
-
         bias_sum = held.tile([P, N], F32, name="bias_sum")
         nc.vector.tensor_tensor(bias_sum[:], both_biases[:, 0, :], both_biases[:, 1, :], mybir.AluOpType.add)
+
+        halves = [psum.tile([P, HALF], F32, name=f"products{h}") for h in range(2)]
+        for l in range(LOADS):
+            for h in range(2):
+                for b in range(l * PER_LOAD, (l + 1) * PER_LOAD):
+                    nc.tensor.matmul(halves[h][:], weight_blocks[:, b, :], x_blocks[b][:, h * HALF : (h + 1) * HALF],
+                                     start=(b == 0), stop=(b == BLOCKS - 1))
+
+        products_sb = held.tile([P, N], F32, name="products_sb")
+        for h in range(2):
+            nc.scalar.activation(products_sb[:, h * HALF : (h + 1) * HALF], halves[h][:], mybir.ActivationFunctionType.Copy)
 
         nc.vector.tensor_tensor(window[:].indirect(offsets[:]), products_sb[:], bias_sum[:], mybir.AluOpType.add)
 

@@ -9,6 +9,7 @@ BLOCKS = R * K // P
 LOADS = 2
 PER_LOAD = BLOCKS // LOADS
 HALF = N // 2
+BURST = 256
 
 FLOPS = 2 * R * K * P * N
 
@@ -17,21 +18,22 @@ def tile_gemmrstritonpcie_kernel(tc, x, weight, bias, base, offs, out):
     nc = tc.nc
     with tc.tile_pool(name="held", bufs=1) as held, tc.psum_pool(name="psum", bufs=1) as psum:
 
+
         offsets = held.tile([P, N // 16], U16, name="offsets")
         nc.sync.dma_start(offsets[:], offs)
 
-        weight_blocks = held.tile([P, BLOCKS, P], BF16, name="weight_blocks")
+        weight_blocks = held.tile([P, BLOCKS, P], BF16, name="weight_blocks", align_bytes=BURST)
         nc.sync.dma_start(weight_blocks[:], weight.flatten_outer_dims().rearrange("(p b) c -> p b c", p=P))
         x_by_load = x.flatten_outer_dims().rearrange("(p l b) n -> l p b n", p=P, l=LOADS)
         x_blocks = []
         for l in range(LOADS):
-            x_part = held.tile([P, PER_LOAD, N], BF16, name=f"x_part{l}")
+            x_part = held.tile([P, PER_LOAD, N], BF16, name=f"x_part{l}", align_bytes=BURST)
             nc.sync.dma_start(x_part[:], x_by_load[l])
             x_blocks.extend(x_part[:, b, :] for b in range(PER_LOAD))
 
-        both_biases = held.tile([P, R, N], F32, name="both_biases")
+        both_biases = held.tile([P, R, N], F32, name="both_biases", align_bytes=BURST)
         nc.sync.dma_start(both_biases[:], bias.rearrange("r c n -> c r n"))
-        window = held.tile([P, S], F32, name="window")
+        window = held.tile([P, S], F32, name="window", align_bytes=BURST)
         nc.sync.dma_start(window[:], base)
 
         bias_sum = held.tile([P, N], F32, name="bias_sum")

@@ -19,9 +19,6 @@ def tile_gemmrstritonpcie_kernel(tc, x, weight, bias, base, offs, out):
     with tc.tile_pool(name="held", bufs=1) as held, tc.psum_pool(name="psum", bufs=1) as psum:
 
 
-        offsets = held.tile([P, N // 16], U16, name="offsets")
-        nc.sync.dma_start(offsets[:], offs)
-
         weight_blocks = held.tile([P, BLOCKS, P], BF16, name="weight_blocks", align_bytes=BURST)
         nc.sync.dma_start(weight_blocks[:], weight.flatten_outer_dims().rearrange("(p b) c -> p b c", p=P))
         x_by_load = x.flatten_outer_dims().rearrange("(p l b) n -> l p b n", p=P, l=LOADS)
@@ -30,6 +27,9 @@ def tile_gemmrstritonpcie_kernel(tc, x, weight, bias, base, offs, out):
             x_part = held.tile([P, PER_LOAD, N], BF16, name=f"x_part{l}", align_bytes=BURST)
             nc.sync.dma_start(x_part[:], x_by_load[l])
             x_blocks.extend(x_part[:, b, :] for b in range(PER_LOAD))
+
+        offsets = held.tile([P, N // 16], U16, name="offsets")
+        nc.sync.dma_start(offsets[:], offs)
 
         both_biases = held.tile([P, R, N], F32, name="both_biases", align_bytes=BURST)
         nc.sync.dma_start(both_biases[:], bias.rearrange("r c n -> c r n"))

@@ -8,6 +8,7 @@ N, S = 512, 1024
 BLOCKS = R * K // P
 LOADS = 2
 PER_LOAD = BLOCKS // LOADS
+WARM_UPS = 6
 HALF = N // 2
 BURST = 256
 
@@ -35,6 +36,12 @@ def tile_gemmrstritonpcie_kernel(tc, x, weight, bias, base, offs, out):
         nc.sync.dma_start(both_biases[:], bias.rearrange("r c n -> c r n"))
         window = held.tile([P, S], F32, name="window", align_bytes=BURST)
         nc.sync.dma_start(window[:], base)
+
+        zeros = held.tile([P, N], BF16, name="zeros")
+        nc.vector.memset(zeros[:], 0.0)
+        unread = psum.tile([P, N], F32, name="unread")
+        for i in range(WARM_UPS):
+            nc.tensor.matmul(unread[:], zeros[:, 0:P], zeros[:], start=True, stop=True)
 
         bias_sum = held.tile([P, N], F32, name="bias_sum")
         nc.vector.tensor_tensor(bias_sum[:], both_biases[:, 0, :], both_biases[:, 1, :], mybir.AluOpType.add)

@@ -6,8 +6,6 @@ P = 128
 R, K = 2, 256
 N, S = 512, 1024
 BLOCKS = R * K // P
-LOADS = 2
-PER_LOAD = BLOCKS // LOADS
 WARM_UPS = 6
 HALF = N // 2
 BURST = 256
@@ -22,12 +20,8 @@ def tile_gemmrstritonpcie_kernel(tc, x, weight, bias, base, offs, out):
 
         weight_blocks = held.tile([P, BLOCKS, P], BF16, name="weight_blocks", align_bytes=BURST)
         nc.sync.dma_start(weight_blocks[:], weight.flatten_outer_dims().rearrange("(p b) c -> p b c", p=P))
-        x_by_load = x.flatten_outer_dims().rearrange("(p l b) n -> l p b n", p=P, l=LOADS)
-        x_blocks = []
-        for l in range(LOADS):
-            x_part = held.tile([P, PER_LOAD, N], BF16, name=f"x_part{l}", align_bytes=BURST)
-            nc.sync.dma_start(x_part[:], x_by_load[l])
-            x_blocks.extend(x_part[:, b, :] for b in range(PER_LOAD))
+        x_blocks = held.tile([P, BLOCKS, N], BF16, name="x_blocks", align_bytes=BURST)
+        nc.sync.dma_start(x_blocks[:], x.flatten_outer_dims().rearrange("(p b) n -> p b n", p=P))
 
         offsets = held.tile([P, N // 16], U16, name="offsets")
         nc.sync.dma_start(offsets[:], offs)
@@ -47,11 +41,10 @@ def tile_gemmrstritonpcie_kernel(tc, x, weight, bias, base, offs, out):
         nc.vector.tensor_tensor(bias_sum[:], both_biases[:, 0, :], both_biases[:, 1, :], mybir.AluOpType.add)
 
         halves = [psum.tile([P, HALF], F32, name=f"products{h}") for h in range(2)]
-        for l in range(LOADS):
-            for h in range(2):
-                for b in range(l * PER_LOAD, (l + 1) * PER_LOAD):
-                    nc.tensor.matmul(halves[h][:], weight_blocks[:, b, :], x_blocks[b][:, h * HALF : (h + 1) * HALF],
-                                     start=(b == 0), stop=(b == BLOCKS - 1))
+        for h in range(2):
+            for b in range(BLOCKS):
+                nc.tensor.matmul(halves[h][:], weight_blocks[:, b, :], x_blocks[:, b, h * HALF : (h + 1) * HALF],
+                                 start=(b == 0), stop=(b == BLOCKS - 1))
 
         products_sb = held.tile([P, N], F32, name="products_sb")
         for h in range(2):

@@ -6,7 +6,7 @@ P = 128
 R, K = 2, 256
 N, S = 512, 1024
 BLOCKS = R * K // P
-WARM_UPS = 6
+WARM_UPS = 4
 HALF = N // 2
 BURST = 256
 

import concourse.mybir as mybir

BF16, F32, U16 = mybir.dt.bfloat16, mybir.dt.float32, mybir.dt.uint16

P = 128
R, K = 2, 256
N, S = 512, 1024
BLOCKS = R * K // P
WARM_UPS = 4
HALF = N // 2
BURST = 256

FLOPS = 2 * R * K * P * N


def tile_gemmrstritonpcie_kernel(tc, x, weight, bias, base, offs, out):
    nc = tc.nc
    with tc.tile_pool(name="held", bufs=1) as held, tc.psum_pool(name="psum", bufs=1) as psum:


        weight_blocks = held.tile([P, BLOCKS, P], BF16, name="weight_blocks", align_bytes=BURST)
        nc.sync.dma_start(weight_blocks[:], weight.flatten_outer_dims().rearrange("(p b) c -> p b c", p=P))
        x_blocks = held.tile([P, BLOCKS, N], BF16, name="x_blocks", align_bytes=BURST)
        nc.sync.dma_start(x_blocks[:], x.flatten_outer_dims().rearrange("(p b) n -> p b n", p=P))

        offsets = held.tile([P, N // 16], U16, name="offsets")
        nc.sync.dma_start(offsets[:], offs)

        both_biases = held.tile([P, R, N], F32, name="both_biases", align_bytes=BURST)
        nc.sync.dma_start(both_biases[:], bias.rearrange("r c n -> c r n"))
        window = held.tile([P, S], F32, name="window", align_bytes=BURST)
        nc.sync.dma_start(window[:], base)

        zeros = held.tile([P, N], BF16, name="zeros")
        nc.vector.memset(zeros[:], 0.0)
        unread = psum.tile([P, N], F32, name="unread")
        for i in range(WARM_UPS):
            nc.tensor.matmul(unread[:], zeros[:, 0:P], zeros[:], start=True, stop=True)

        bias_sum = held.tile([P, N], F32, name="bias_sum")
        nc.vector.tensor_tensor(bias_sum[:], both_biases[:, 0, :], both_biases[:, 1, :], mybir.AluOpType.add)

        halves = [psum.tile([P, HALF], F32, name=f"products{h}") for h in range(2)]
        for h in range(2):
            for b in range(BLOCKS):
                nc.tensor.matmul(halves[h][:], weight_blocks[:, b, :], x_blocks[:, b, h * HALF : (h + 1) * HALF],
                                 start=(b == 0), stop=(b == BLOCKS - 1))

        products_sb = held.tile([P, N], F32, name="products_sb")
        for h in range(2):
            nc.scalar.activation(products_sb[:, h * HALF : (h + 1) * HALF], halves[h][:], mybir.ActivationFunctionType.Copy)

        nc.vector.tensor_tensor(window[:].indirect(offsets[:]), products_sb[:], bias_sum[:], mybir.AluOpType.add)

        nc.sync.dma_start(out, window[:])
